import numpy as np
import ml_dtypes


def mxq(x, axis, fmt="e4m3"):
    dtype, down = {"e4m3": (ml_dtypes.float8_e4m3fn, 7), "e5m2": (ml_dtypes.float8_e5m2, 14)}[fmt]
    v = np.moveaxis(np.asarray(x, np.float32).astype(ml_dtypes.bfloat16).astype(np.float64), axis, -1)
    blocks = v.reshape(v.shape[:-1] + (-1, 32))
    amax = np.abs(blocks).max(-1, keepdims=True)
    byte = np.maximum(np.where(amax > 0, np.frexp(amax)[1] - 1 + 127, 0) - down, 1)
    scale = np.exp2(byte - 127.0)
    codes = (blocks / scale).astype(np.float32).astype(dtype).astype(np.float64)
    return np.moveaxis((codes * scale).reshape(v.shape), -1, axis)


WIDE = False


def mx_kscale(k):
    if not WIDE:
        return np.ones(k)
    levels = np.array([10, -10, 5, -5, 0])
    a = np.random.permutation(np.resize(levels, k // 512 * 4)).reshape(k // 512, 4)
    idx = np.arange(k)
    return np.exp2(a[idx // 512, idx % 128 // 32])


BF16 = ml_dtypes.bfloat16


def bf(x):
    return np.asarray(x, np.float32).astype(BF16)


def f64(x):
    return np.asarray(x).astype(np.float64)


B, S, D, HD, M = 4, 128, 16384, 128, 4
N = S // M
NEG = float(np.finfo(np.float32).min)


def prev(x):
    return np.concatenate([np.zeros_like(x[:, :1]), x[:, :-1]], axis=1)


def setup_inputs():
    s = mx_kscale(D)

    def w():
        return bf(np.random.standard_normal((D, HD)) / np.sqrt(D) / s[:, None])

    return {"h": bf(np.random.standard_normal((B, S, D)) * s),
            "w_kv_a": w(), "w_kv_b": w(), "w_z_a": w(), "w_z_b": w(),
            "b_a": bf(np.random.standard_normal((M, HD)) * 0.5),
            "b_b": bf(np.random.standard_normal((M, HD)) * 0.5)}


def reference(h, w_kv_a, w_kv_b, w_z_a, w_z_b, b_a, b_b):
    hq = mxq(f64(h), 2, "e4m3")
    c_a = (hq @ mxq(f64(w_kv_a), 0, "e4m3")).reshape(B, N, M, HD)
    c_b = (hq @ mxq(f64(w_kv_b), 0, "e4m3")).reshape(B, N, M, HD)
    z_a = (hq @ mxq(f64(w_z_a), 0, "e4m3")).reshape(B, N, M, HD)
    z_b = (hq @ mxq(f64(w_z_b), 0, "e4m3")).reshape(B, N, M, HD)
    logits = np.concatenate([prev(z_b) + f64(b_b), z_a + f64(b_a)], axis=2)
    valid = np.concatenate([np.broadcast_to((np.arange(N) > 0)[:, None], (N, M)), np.ones((N, M), bool)], axis=1)
    logits = np.where(valid[None, :, :, None], logits, NEG)
    e = np.exp(logits - logits.max(axis=2, keepdims=True))
    weights = e / e.sum(axis=2, keepdims=True)
    c_vals = np.concatenate([prev(c_b), c_a], axis=2)
    return np.sum(weights * c_vals, axis=2)

@@ -1,0 +1,236 @@
+from contextlib import ExitStack
+
+import concourse.mybir as mybir
+from concourse.masks import make_identity
+
+F32 = mybir.dt.float32
+BF16 = mybir.dt.bfloat16
+U32 = mybir.dt.uint32
+U8 = mybir.dt.uint8
+FP8X4 = mybir.dt.float8_e4m3fn_x4
+ALU = mybir.AluOpType
+ACT = mybir.ActivationFunctionType
+AXIS = mybir.AxisListType
+
+P = 128
+PACK = 4
+K_PASS = P * PACK
+
+SEQS = 4
+SEQ_LEN = 128
+D = 16384
+FEATURES = 128
+BLOCK_LEN = 4
+TOKENS = SEQS * SEQ_LEN
+BLOCKS = SEQ_LEN // BLOCK_LEN
+WINDOW = 2 * BLOCK_LEN
+PASSES = D // K_PASS
+CHUNK_PASSES = 4
+CHUNKS = PASSES // CHUNK_PASSES
+CHUNK_K = CHUNK_PASSES * K_PASS
+ROUND_PASSES = 2
+WORDS_PASS = K_PASS // 2
+BANK_TOKENS = 2 * SEQ_LEN
+NEG = -3.4028234663852886e38
+
+FLOPS = 2 * TOKENS * D * 4 * FEATURES
+
+
+def load_weight_chunk(nc, pool, weight, c):
+    w_raw = pool.tile([P, CHUNK_PASSES, PACK * FEATURES], BF16)
+    rows = weight[c * CHUNK_K : (c + 1) * CHUNK_K, :]
+    nc.sync.dma_start(out=w_raw[:], in_=rows.rearrange("(g p t) n -> p g (t n)", p=P, t=PACK))
+    return w_raw
+
+
+def quantise_weight_chunk(nc, grouped_pool, packed_pool, w_raw, on_vector):
+    w_grouped = grouped_pool.tile([P, CHUNK_PASSES, FEATURES, PACK], BF16, align_bytes=64)
+    if on_vector:
+        nc.vector.tensor_copy(
+            out=w_grouped[:].rearrange("p g (c i) t -> p g c t i", i=4),
+            in_=w_raw[:].rearrange("p g (t c i) -> p g c t i", t=PACK, i=4),
+        )
+    else:
+        nc.scalar.copy(out=w_grouped[:], in_=w_raw[:].rearrange("p g (t n) -> p g n t", t=PACK))
+    w_codes = packed_pool.tile([P, CHUNK_PASSES, FEATURES], U32, align_bytes=64)
+    w_scales = packed_pool.tile([P, CHUNK_PASSES, FEATURES], U8, align_bytes=64)
+    nc.vector.quantize_mx(
+        out=w_codes[:].rearrange("p g n -> p (g n)").bitcast(FP8X4),
+        scales=w_scales[:].rearrange("p g n -> p (g n)"),
+        in_=w_grouped[:].rearrange("p g n t -> p (g n t)"),
+    )
+    return w_codes, w_scales
+
+
+def tile_tokenlevelcompressor_pa_k_kernel(tc, h, w_kv_a, w_kv_b, w_z_a, w_z_b, b_a, b_b, out):
+    nc = tc.nc
+    with ExitStack() as stack:
+        const = stack.enter_context(tc.tile_pool(name="const", bufs=1))
+        keep = stack.enter_context(tc.tile_pool(name="keep", bufs=1))
+        h_in = stack.enter_context(tc.tile_pool(name="h_in", bufs=3))
+        h_group = stack.enter_context(tc.tile_pool(name="h_group", bufs=4))
+        w_in = stack.enter_context(tc.tile_pool(name="w_in", bufs=6))
+        w_group = stack.enter_context(tc.tile_pool(name="w_group", bufs=3))
+        w_packed = stack.enter_context(tc.tile_pool(name="w_packed", bufs=6))
+        soft = stack.enter_context(tc.tile_pool(name="soft", bufs=1))
+        sums = stack.enter_context(tc.psum_pool(name="sums", bufs=1))
+        banks = stack.enter_context(tc.psum_pool(name="banks", bufs=4))
+
+        ident = const.tile([P, P], F32)
+        make_identity(nc, ident[:])
+
+        warm = const.tile([P, 1], F32)
+        nc.vector.memset(warm[:], 0.0)
+        nc.scalar.activation(out=warm[:], in_=warm[:], func=ACT.Exp)
+
+        bias_rows = const.tile([P, FEATURES], BF16)
+        nc.vector.memset(bias_rows[:], 0.0)
+        nc.scalar.dma_start(out=bias_rows[0:BLOCK_LEN, :], in_=b_b)
+        nc.scalar.dma_start(out=bias_rows[BLOCK_LEN:WINDOW, :], in_=b_a)
+        bias_rows_f32 = const.tile([P, FEATURES], F32)
+        nc.vector.tensor_copy(out=bias_rows_f32[:], in_=bias_rows[:])
+
+        logits = soft.tile([P, SEQS, BLOCKS, WINDOW], F32)
+        products = soft.tile([P, SEQS, BLOCKS, WINDOW], F32)
+        nc.vector.memset(logits[:, :, 0:1, 0:BLOCK_LEN], NEG)
+        nc.vector.memset(products[:, :, 0:1, 0:BLOCK_LEN], 0.0)
+
+        h_codes = keep.tile([P, PASSES, TOKENS], U32, align_bytes=64)
+        h_scales = keep.tile([P, PASSES, TOKENS], U8, align_bytes=64)
+
+        z_a = sums.tile([P, TOKENS], F32)
+        z_b = sums.tile([P, TOKENS], F32)
+        c_a = sums.tile([P, TOKENS], F32)
+        c_b = sums.tile([P, TOKENS], F32)
+
+        def project(passes, pairs):
+            for acc, w_codes, w_scales in pairs:
+                for g in passes:
+                    nc.tensor.matmul_mx(
+                        out=acc[:],
+                        lhsT=w_codes[:, g % CHUNK_PASSES, :].bitcast(FP8X4),
+                        lhsT_scale=w_scales[:, g % CHUNK_PASSES, :],
+                        rhs=h_codes[:, g, :].bitcast(FP8X4),
+                        rhs_scale=h_scales[:, g, :],
+                        start=(g == 0),
+                        stop=(g == PASSES - 1),
+                    )
+
+        tokens_first = h.rearrange("b s d -> s b d")
+        waiting = None
+        for c in range(CHUNKS):
+            h_raw = h_in.tile([P, SEQS, CHUNK_K], BF16)
+            nc.sync.dma_start(out=h_raw[:], in_=tokens_first[:, :, c * CHUNK_K : (c + 1) * CHUNK_K])
+            z_a_raw = load_weight_chunk(nc, w_in, w_z_a, c)
+            z_b_raw = load_weight_chunk(nc, w_in, w_z_b, c)
+            z_a_codes, z_a_scales = quantise_weight_chunk(nc, w_group, w_packed, z_a_raw, True)
+            z_b_codes, z_b_scales = quantise_weight_chunk(nc, w_group, w_packed, z_b_raw, True)
+            pairs = [(z_a, z_a_codes, z_a_scales), (z_b, z_b_codes, z_b_scales)]
+
+            for first in range(0, CHUNK_PASSES, ROUND_PASSES):
+                local_passes = range(first, first + ROUND_PASSES)
+                grouped_tiles = []
+                for gl in local_passes:
+                    h_grouped = h_group.tile([P, TOKENS, PACK], BF16, align_bytes=64)
+                    grouped_words = (
+                        h_grouped[:]
+                        .rearrange("p n t -> p (n t)")
+                        .bitcast(F32)
+                        .rearrange("p (n u) -> p n u", u=2)
+                    )
+                    for half in range(TOKENS // BANK_TOKENS):
+                        bank = banks.tile([P, 2, BANK_TOKENS], F32)
+                        for u in range(2):
+                            for s in range(2):
+                                words = h_raw[:, 2 * half + s, :].bitcast(F32)
+                                nc.tensor.transpose(
+                                    bank[:, u, s * SEQ_LEN : (s + 1) * SEQ_LEN],
+                                    words[:, gl * WORDS_PASS + u : (gl + 1) * WORDS_PASS : 2],
+                                    ident[:],
+                                )
+                        nc.scalar.copy(
+                            out=grouped_words[:, half * BANK_TOKENS : (half + 1) * BANK_TOKENS, :],
+                            in_=bank[:].rearrange("p u n -> p n u"),
+                        )
+                    grouped_tiles.append(h_grouped)
+                for gl, h_grouped in zip(local_passes, grouped_tiles):
+                    g = c * CHUNK_PASSES + gl
+                    nc.vector.quantize_mx(
+                        out=h_codes[:, g, :].bitcast(FP8X4),
+                        scales=h_scales[:, g, :],
+                        in_=h_grouped[:].rearrange("p n t -> p (n t)"),
+                    )
+                if waiting is not None:
+                    project(waiting[0], waiting[1])
+                waiting = ([c * CHUNK_PASSES + gl for gl in local_passes], pairs)
+        project(waiting[0], waiting[1])
+
+        bias_bank = banks.tile([P, 2, BANK_TOKENS], F32, name="bank")
+        nc.tensor.transpose(bias_bank[:, 0, 0:P], bias_rows_f32[:], ident[:])
+        bias = const.tile([P, WINDOW], F32)
+        nc.vector.tensor_copy(out=bias[:], in_=bias_bank[:, 0, 0:WINDOW])
+        by_block = "p (b j i) -> p b j i"
+        nc.vector.tensor_tensor(
+            out=logits[:, :, 1:BLOCKS, 0:BLOCK_LEN],
+            in0=z_b[:].rearrange(by_block, b=SEQS, i=BLOCK_LEN)[:, :, 0 : BLOCKS - 1, :],
+            in1=bias[:, 0:BLOCK_LEN].unsqueeze(1).unsqueeze(1).to_broadcast([P, SEQS, BLOCKS - 1, BLOCK_LEN]),
+            op=ALU.add,
+        )
+        nc.vector.tensor_tensor(
+            out=logits[:, :, :, BLOCK_LEN:WINDOW],
+            in0=z_a[:].rearrange(by_block, b=SEQS, i=BLOCK_LEN),
+            in1=bias[:, BLOCK_LEN:WINDOW].unsqueeze(1).unsqueeze(1).to_broadcast([P, SEQS, BLOCKS, BLOCK_LEN]),
+            op=ALU.add,
+        )
+        windows = logits[:].rearrange("p b j s -> p (b j) s")
+        top = soft.tile([P, SEQS * BLOCKS], F32)
+        nc.vector.tensor_reduce(out=top[:], in_=windows, axis=AXIS.X, op=ALU.max)
+        nc.vector.tensor_tensor(
+            out=windows,
+            in0=windows,
+            in1=top[:].unsqueeze(2).to_broadcast([P, SEQS * BLOCKS, WINDOW]),
+            op=ALU.subtract,
+        )
+        expd = soft.tile([P, SEQS, BLOCKS, WINDOW], F32)
+        nc.scalar.activation(out=expd[:], in_=logits[:], func=ACT.Exp)
+        denom = soft.tile([P, SEQS * BLOCKS], F32)
+        nc.vector.tensor_reduce(
+            out=denom[:], in_=expd[:].rearrange("p b j s -> p (b j) s"), axis=AXIS.X, op=ALU.add
+        )
+        inv_denom = soft.tile([P, SEQS * BLOCKS], F32)
+        nc.vector.reciprocal(out=inv_denom[:], in_=denom[:])
+
+        for c in range(CHUNKS):
+            c_a_raw = load_weight_chunk(nc, w_in, w_kv_a, c)
+            c_b_raw = load_weight_chunk(nc, w_in, w_kv_b, c)
+            c_b_codes, c_b_scales = quantise_weight_chunk(nc, w_group, w_packed, c_b_raw, False)
+            c_a_codes, c_a_scales = quantise_weight_chunk(nc, w_group, w_packed, c_a_raw, True)
+            project(
+                range(c * CHUNK_PASSES, (c + 1) * CHUNK_PASSES),
+                [(c_b, c_b_codes, c_b_scales), (c_a, c_a_codes, c_a_scales)],
+            )
+
+        nc.vector.tensor_tensor(
+            out=products[:, :, 1:BLOCKS, 0:BLOCK_LEN],
+            in0=c_b[:].rearrange(by_block, b=SEQS, i=BLOCK_LEN)[:, :, 0 : BLOCKS - 1, :],
+            in1=expd[:, :, 1:BLOCKS, 0:BLOCK_LEN],
+            op=ALU.mult,
+        )
+        nc.vector.tensor_tensor(
+            out=products[:, :, :, BLOCK_LEN:WINDOW],
+            in0=c_a[:].rearrange(by_block, b=SEQS, i=BLOCK_LEN),
+            in1=expd[:, :, :, BLOCK_LEN:WINDOW],
+            op=ALU.mult,
+        )
+        numer = soft.tile([P, SEQS * BLOCKS], F32)
+        nc.vector.tensor_reduce(
+            out=numer[:], in_=products[:].rearrange("p b j s -> p (b j) s"), axis=AXIS.X, op=ALU.add
+        )
+        result = soft.tile([P, SEQS * BLOCKS], F32)
+        nc.vector.tensor_tensor(out=result[:], in0=numer[:], in1=inv_denom[:], op=ALU.mult)
+
+        result_bank = banks.tile([P, 2, BANK_TOKENS], F32, name="bank")
+        nc.tensor.transpose(result_bank[:, 0, 0:P], result[:], ident[:])
+        rows_out = soft.tile([P, FEATURES], F32)
+        nc.vector.tensor_copy(out=rows_out[:], in_=result_bank[:, 0, 0:P])
+        nc.sync.dma_start(out=out.rearrange("b j f -> (b j) f"), in_=rows_out[:])

@@ -29,37 +29,15 @@ CHUNK_PASSES = 4
 CHUNKS = PASSES // CHUNK_PASSES
 CHUNK_K = CHUNK_PASSES * K_PASS
 ROUND_PASSES = 2
+CHUNK_ROUNDS = CHUNK_PASSES // ROUND_PASSES
+LAG = 4
+assert LAG >= 2
+ROUNDS = (CHUNKS + LAG) * CHUNK_ROUNDS
 WORDS_PASS = K_PASS // 2
 BANK_TOKENS = 2 * SEQ_LEN
 NEG = -3.4028234663852886e38
 
 FLOPS = 2 * TOKENS * D * 4 * FEATURES
-
-
-def load_weight_chunk(nc, pool, weight, c):
-    w_raw = pool.tile([P, CHUNK_PASSES, PACK * FEATURES], BF16)
-    rows = weight[c * CHUNK_K : (c + 1) * CHUNK_K, :]
-    nc.sync.dma_start(out=w_raw[:], in_=rows.rearrange("(g p t) n -> p g (t n)", p=P, t=PACK))
-    return w_raw
-
-
-def quantise_weight_chunk(nc, grouped_pool, packed_pool, w_raw, on_vector):
-    w_grouped = grouped_pool.tile([P, CHUNK_PASSES, FEATURES, PACK], BF16, align_bytes=64)
-    if on_vector:
-        nc.vector.tensor_copy(
-            out=w_grouped[:].rearrange("p g (c i) t -> p g c t i", i=4),
-            in_=w_raw[:].rearrange("p g (t c i) -> p g c t i", t=PACK, i=4),
-        )
-    else:
-        nc.scalar.copy(out=w_grouped[:], in_=w_raw[:].rearrange("p g (t n) -> p g n t", t=PACK))
-    w_codes = packed_pool.tile([P, CHUNK_PASSES, FEATURES], U32, align_bytes=64)
-    w_scales = packed_pool.tile([P, CHUNK_PASSES, FEATURES], U8, align_bytes=64)
-    nc.vector.quantize_mx(
-        out=w_codes[:].rearrange("p g n -> p (g n)").bitcast(FP8X4),
-        scales=w_scales[:].rearrange("p g n -> p (g n)"),
-        in_=w_grouped[:].rearrange("p g n t -> p (g n t)"),
-    )
-    return w_codes, w_scales
 
 
 def tile_tokenlevelcompressor_pa_k_kernel(tc, h, w_kv_a, w_kv_b, w_z_a, w_z_b, b_a, b_b, out):
@@ -69,26 +47,54 @@ def tile_tokenlevelcompressor_pa_k_kernel(tc, h, w_kv_a, w_kv_b, w_z_a, w_z_b, b
         keep = stack.enter_context(tc.tile_pool(name="keep", bufs=1))
         h_in = stack.enter_context(tc.tile_pool(name="h_in", bufs=3))
         h_group = stack.enter_context(tc.tile_pool(name="h_group", bufs=4))
-        w_in = stack.enter_context(tc.tile_pool(name="w_in", bufs=6))
-        w_group = stack.enter_context(tc.tile_pool(name="w_group", bufs=3))
-        w_packed = stack.enter_context(tc.tile_pool(name="w_packed", bufs=6))
+        w_in = stack.enter_context(tc.tile_pool(name="w_in", bufs=8))
+        w_group = stack.enter_context(tc.tile_pool(name="w_group", bufs=4))
+        w_packed = stack.enter_context(tc.tile_pool(name="w_packed", bufs=8))
         soft = stack.enter_context(tc.tile_pool(name="soft", bufs=1))
         sums = stack.enter_context(tc.psum_pool(name="sums", bufs=1))
         banks = stack.enter_context(tc.psum_pool(name="banks", bufs=4))
+        stack.enter_context(tc.manual_schedule())
+
+        def load_weight_chunk(weight, c):
+            w_raw = w_in.tile([P, CHUNK_PASSES, PACK * FEATURES], BF16)
+            rows = weight[c * CHUNK_K : (c + 1) * CHUNK_K, :]
+            nc.sync.dma_start(out=w_raw[:], in_=rows.rearrange("(g p t) n -> p g (t n)", p=P, t=PACK))
+            return w_raw
+
+        def regroup_on_vector(w_raw):
+            w_grouped = w_group.tile([P, CHUNK_PASSES, FEATURES, PACK], BF16, align_bytes=64)
+            nc.vector.tensor_copy(
+                out=w_grouped[:].rearrange("p g (c i) t -> p g c t i", i=4),
+                in_=w_raw[:].rearrange("p g (t c i) -> p g c t i", t=PACK, i=4),
+            )
+            return w_grouped
+
+        def regroup_on_scalar(w_raw):
+            w_grouped = w_group.tile([P, CHUNK_PASSES, FEATURES, PACK], BF16, align_bytes=64)
+            nc.scalar.copy(out=w_grouped[:], in_=w_raw[:].rearrange("p g (t n) -> p g n t", t=PACK))
+            return w_grouped
+
+        def quantise_weight_chunk(w_grouped):
+            w_codes = w_packed.tile([P, CHUNK_PASSES, FEATURES], U32, align_bytes=64)
+            w_scales = w_packed.tile([P, CHUNK_PASSES, FEATURES], U8, align_bytes=64)
+            nc.vector.quantize_mx(
+                out=w_codes[:].rearrange("p g n -> p (g n)").bitcast(FP8X4),
+                scales=w_scales[:].rearrange("p g n -> p (g n)"),
+                in_=w_grouped[:].rearrange("p g n t -> p (g n t)"),
+            )
+            return w_codes, w_scales
 
         ident = const.tile([P, P], F32)
         make_identity(nc, ident[:])
-
-        warm = const.tile([P, 1], F32)
-        nc.vector.memset(warm[:], 0.0)
-        nc.scalar.activation(out=warm[:], in_=warm[:], func=ACT.Exp)
 
         bias_rows = const.tile([P, FEATURES], BF16)
         nc.vector.memset(bias_rows[:], 0.0)
         nc.scalar.dma_start(out=bias_rows[0:BLOCK_LEN, :], in_=b_b)
         nc.scalar.dma_start(out=bias_rows[BLOCK_LEN:WINDOW, :], in_=b_a)
-        bias_rows_f32 = const.tile([P, FEATURES], F32)
-        nc.vector.tensor_copy(out=bias_rows_f32[:], in_=bias_rows[:])
+
+        warm = const.tile([P, 1], F32)
+        nc.vector.memset(warm[:], 0.0)
+        nc.scalar.activation(out=warm[:], in_=warm[:], func=ACT.Exp)
 
         logits = soft.tile([P, SEQS, BLOCKS, WINDOW], F32)
         products = soft.tile([P, SEQS, BLOCKS, WINDOW], F32)
@@ -103,112 +109,153 @@ def tile_tokenlevelcompressor_pa_k_kernel(tc, h, w_kv_a, w_kv_b, w_z_a, w_z_b, b
         c_a = sums.tile([P, TOKENS], F32)
         c_b = sums.tile([P, TOKENS], F32)
 
-        def project(passes, pairs):
-            for acc, w_codes, w_scales in pairs:
-                for g in passes:
+        tokens_first = h.rearrange("b s d -> s b d")
+        h_raw_of = {}
+        raw_of = {}
+        packed_of = {}
+
+        def load_step(c):
+            if c < CHUNKS:
+                raw_of["z", c] = (load_weight_chunk(w_z_a, c), load_weight_chunk(w_z_b, c))
+            if 0 <= c - LAG < CHUNKS:
+                raw_of["kv", c - LAG] = (load_weight_chunk(w_kv_a, c - LAG), load_weight_chunk(w_kv_b, c - LAG))
+            if c < CHUNKS:
+                h_raw = h_in.tile([P, SEQS, CHUNK_K], BF16)
+                nc.sync.dma_start(out=h_raw[:], in_=tokens_first[:, :, c * CHUNK_K : (c + 1) * CHUNK_K])
+                h_raw_of[c] = h_raw
+
+        def prepare_logit_weights(c):
+            raw_a, raw_b = raw_of["z", c]
+            grouped_a = regroup_on_vector(raw_a)
+            grouped_b = regroup_on_vector(raw_b)
+            codes_a, scales_a = quantise_weight_chunk(grouped_a)
+            codes_b, scales_b = quantise_weight_chunk(grouped_b)
+            packed_of["z", c] = [(z_a, codes_a, scales_a), (z_b, codes_b, scales_b)]
+
+        def prepare_value_weights(c):
+            raw_a, raw_b = raw_of["kv", c]
+            grouped_b = regroup_on_scalar(raw_b)
+            grouped_a = regroup_on_vector(raw_a)
+            codes_a, scales_a = quantise_weight_chunk(grouped_a)
+            codes_b, scales_b = quantise_weight_chunk(grouped_b)
+            packed_of["kv", c] = [(c_b, codes_b, scales_b), (c_a, codes_a, scales_a)]
+
+        def quantise_h_round(c, r):
+            h_raw = h_raw_of[c]
+            local_passes = range(r * ROUND_PASSES, (r + 1) * ROUND_PASSES)
+            grouped_tiles = []
+            for gl in local_passes:
+                h_grouped = h_group.tile([P, TOKENS, PACK], BF16, align_bytes=64)
+                grouped_words = (
+                    h_grouped[:].rearrange("p n t -> p (n t)").bitcast(F32).rearrange("p (n u) -> p n u", u=2)
+                )
+                for half in range(TOKENS // BANK_TOKENS):
+                    bank = banks.tile([P, 2, BANK_TOKENS], F32)
+                    for u in range(2):
+                        for s in range(2):
+                            words = h_raw[:, 2 * half + s, :].bitcast(F32)
+                            nc.tensor.transpose(
+                                bank[:, u, s * SEQ_LEN : (s + 1) * SEQ_LEN],
+                                words[:, gl * WORDS_PASS + u : (gl + 1) * WORDS_PASS : 2],
+                                ident[:],
+                            )
+                    nc.scalar.copy(
+                        out=grouped_words[:, half * BANK_TOKENS : (half + 1) * BANK_TOKENS, :],
+                        in_=bank[:].rearrange("p u n -> p n u"),
+                    )
+                grouped_tiles.append(h_grouped)
+            for gl, h_grouped in zip(local_passes, grouped_tiles):
+                g = c * CHUNK_PASSES + gl
+                nc.vector.quantize_mx(
+                    out=h_codes[:, g, :].bitcast(FP8X4),
+                    scales=h_scales[:, g, :],
+                    in_=h_grouped[:].rearrange("p n t -> p (n t)"),
+                )
+
+        def project(kind, c, r):
+            for acc, w_codes, w_scales in packed_of[kind, c]:
+                for gl in range(r * ROUND_PASSES, (r + 1) * ROUND_PASSES):
+                    g = c * CHUNK_PASSES + gl
                     nc.tensor.matmul_mx(
                         out=acc[:],
-                        lhsT=w_codes[:, g % CHUNK_PASSES, :].bitcast(FP8X4),
-                        lhsT_scale=w_scales[:, g % CHUNK_PASSES, :],
+                        lhsT=w_codes[:, gl, :].bitcast(FP8X4),
+                        lhsT_scale=w_scales[:, gl, :],
                         rhs=h_codes[:, g, :].bitcast(FP8X4),
                         rhs_scale=h_scales[:, g, :],
                         start=(g == 0),
                         stop=(g == PASSES - 1),
                     )
 
-        tokens_first = h.rearrange("b s d -> s b d")
-        waiting = None
-        for c in range(CHUNKS):
-            h_raw = h_in.tile([P, SEQS, CHUNK_K], BF16)
-            nc.sync.dma_start(out=h_raw[:], in_=tokens_first[:, :, c * CHUNK_K : (c + 1) * CHUNK_K])
-            z_a_raw = load_weight_chunk(nc, w_in, w_z_a, c)
-            z_b_raw = load_weight_chunk(nc, w_in, w_z_b, c)
-            z_a_codes, z_a_scales = quantise_weight_chunk(nc, w_group, w_packed, z_a_raw, True)
-            z_b_codes, z_b_scales = quantise_weight_chunk(nc, w_group, w_packed, z_b_raw, True)
-            pairs = [(z_a, z_a_codes, z_a_scales), (z_b, z_b_codes, z_b_scales)]
+        by_block = "p (b j i) -> p b j i"
+        windows = logits[:].rearrange("p b j s -> p (b j) s")
+        bias = const.tile([P, WINDOW], F32)
+        top = soft.tile([P, SEQS * BLOCKS], F32)
+        expd = soft.tile([P, SEQS, BLOCKS, WINDOW], F32)
+        denom = soft.tile([P, SEQS * BLOCKS], F32)
+        inv_denom = soft.tile([P, SEQS * BLOCKS], F32)
 
-            for first in range(0, CHUNK_PASSES, ROUND_PASSES):
-                local_passes = range(first, first + ROUND_PASSES)
-                grouped_tiles = []
-                for gl in local_passes:
-                    h_grouped = h_group.tile([P, TOKENS, PACK], BF16, align_bytes=64)
-                    grouped_words = (
-                        h_grouped[:]
-                        .rearrange("p n t -> p (n t)")
-                        .bitcast(F32)
-                        .rearrange("p (n u) -> p n u", u=2)
-                    )
-                    for half in range(TOKENS // BANK_TOKENS):
-                        bank = banks.tile([P, 2, BANK_TOKENS], F32)
-                        for u in range(2):
-                            for s in range(2):
-                                words = h_raw[:, 2 * half + s, :].bitcast(F32)
-                                nc.tensor.transpose(
-                                    bank[:, u, s * SEQ_LEN : (s + 1) * SEQ_LEN],
-                                    words[:, gl * WORDS_PASS + u : (gl + 1) * WORDS_PASS : 2],
-                                    ident[:],
-                                )
-                        nc.scalar.copy(
-                            out=grouped_words[:, half * BANK_TOKENS : (half + 1) * BANK_TOKENS, :],
-                            in_=bank[:].rearrange("p u n -> p n u"),
-                        )
-                    grouped_tiles.append(h_grouped)
-                for gl, h_grouped in zip(local_passes, grouped_tiles):
-                    g = c * CHUNK_PASSES + gl
-                    nc.vector.quantize_mx(
-                        out=h_codes[:, g, :].bitcast(FP8X4),
-                        scales=h_scales[:, g, :],
-                        in_=h_grouped[:].rearrange("p n t -> p (n t)"),
-                    )
-                if waiting is not None:
-                    project(waiting[0], waiting[1])
-                waiting = ([c * CHUNK_PASSES + gl for gl in local_passes], pairs)
-        project(waiting[0], waiting[1])
+        def shifted_logits():
+            nc.vector.tensor_tensor(
+                out=logits[:, :, 1:BLOCKS, 0:BLOCK_LEN],
+                in0=z_b[:].rearrange(by_block, b=SEQS, i=BLOCK_LEN)[:, :, 0 : BLOCKS - 1, :],
+                in1=bias[:, 0:BLOCK_LEN].unsqueeze(1).unsqueeze(1).to_broadcast([P, SEQS, BLOCKS - 1, BLOCK_LEN]),
+                op=ALU.add,
+            )
+            nc.vector.tensor_tensor(
+                out=logits[:, :, :, BLOCK_LEN:WINDOW],
+                in0=z_a[:].rearrange(by_block, b=SEQS, i=BLOCK_LEN),
+                in1=bias[:, BLOCK_LEN:WINDOW].unsqueeze(1).unsqueeze(1).to_broadcast([P, SEQS, BLOCKS, BLOCK_LEN]),
+                op=ALU.add,
+            )
+            nc.vector.tensor_reduce(out=top[:], in_=windows, axis=AXIS.X, op=ALU.max)
+            nc.vector.tensor_tensor(
+                out=windows,
+                in0=windows,
+                in1=top[:].unsqueeze(2).to_broadcast([P, SEQS * BLOCKS, WINDOW]),
+                op=ALU.subtract,
+            )
 
+        def exponentials():
+            nc.scalar.activation(out=expd[:], in_=logits[:], func=ACT.Exp)
+
+        def denominators():
+            nc.vector.tensor_reduce(
+                out=denom[:], in_=expd[:].rearrange("p b j s -> p (b j) s"), axis=AXIS.X, op=ALU.add
+            )
+            nc.vector.reciprocal(out=inv_denom[:], in_=denom[:])
+
+        load_step(0)
+        prepare_logit_weights(0)
+
+        bias_rows_f32 = const.tile([P, FEATURES], F32)
+        nc.vector.tensor_copy(out=bias_rows_f32[:], in_=bias_rows[:])
         bias_bank = banks.tile([P, 2, BANK_TOKENS], F32, name="bank")
         nc.tensor.transpose(bias_bank[:, 0, 0:P], bias_rows_f32[:], ident[:])
-        bias = const.tile([P, WINDOW], F32)
         nc.vector.tensor_copy(out=bias[:], in_=bias_bank[:, 0, 0:WINDOW])
-        by_block = "p (b j i) -> p b j i"
-        nc.vector.tensor_tensor(
-            out=logits[:, :, 1:BLOCKS, 0:BLOCK_LEN],
-            in0=z_b[:].rearrange(by_block, b=SEQS, i=BLOCK_LEN)[:, :, 0 : BLOCKS - 1, :],
-            in1=bias[:, 0:BLOCK_LEN].unsqueeze(1).unsqueeze(1).to_broadcast([P, SEQS, BLOCKS - 1, BLOCK_LEN]),
-            op=ALU.add,
-        )
-        nc.vector.tensor_tensor(
-            out=logits[:, :, :, BLOCK_LEN:WINDOW],
-            in0=z_a[:].rearrange(by_block, b=SEQS, i=BLOCK_LEN),
-            in1=bias[:, BLOCK_LEN:WINDOW].unsqueeze(1).unsqueeze(1).to_broadcast([P, SEQS, BLOCKS, BLOCK_LEN]),
-            op=ALU.add,
-        )
-        windows = logits[:].rearrange("p b j s -> p (b j) s")
-        top = soft.tile([P, SEQS * BLOCKS], F32)
-        nc.vector.tensor_reduce(out=top[:], in_=windows, axis=AXIS.X, op=ALU.max)
-        nc.vector.tensor_tensor(
-            out=windows,
-            in0=windows,
-            in1=top[:].unsqueeze(2).to_broadcast([P, SEQS * BLOCKS, WINDOW]),
-            op=ALU.subtract,
-        )
-        expd = soft.tile([P, SEQS, BLOCKS, WINDOW], F32)
-        nc.scalar.activation(out=expd[:], in_=logits[:], func=ACT.Exp)
-        denom = soft.tile([P, SEQS * BLOCKS], F32)
-        nc.vector.tensor_reduce(
-            out=denom[:], in_=expd[:].rearrange("p b j s -> p (b j) s"), axis=AXIS.X, op=ALU.add
-        )
-        inv_denom = soft.tile([P, SEQS * BLOCKS], F32)
-        nc.vector.reciprocal(out=inv_denom[:], in_=denom[:])
 
-        for c in range(CHUNKS):
-            c_a_raw = load_weight_chunk(nc, w_in, w_kv_a, c)
-            c_b_raw = load_weight_chunk(nc, w_in, w_kv_b, c)
-            c_b_codes, c_b_scales = quantise_weight_chunk(nc, w_group, w_packed, c_b_raw, False)
-            c_a_codes, c_a_scales = quantise_weight_chunk(nc, w_group, w_packed, c_a_raw, True)
-            project(
-                range(c * CHUNK_PASSES, (c + 1) * CHUNK_PASSES),
-                [(c_b, c_b_codes, c_b_scales), (c_a, c_a_codes, c_a_scales)],
-            )
+        logits_done = CHUNKS * CHUNK_ROUNDS
+        for t in range(ROUNDS + 1):
+            c, r = divmod(t, CHUNK_ROUNDS)
+            if r == 0:
+                load_step(c + 1)
+            if c < CHUNKS:
+                quantise_h_round(c, r)
+            if t >= 1:
+                before_c, before_r = divmod(t - 1, CHUNK_ROUNDS)
+                if before_c < CHUNKS:
+                    project("z", before_c, before_r)
+                if 0 <= before_c - LAG < CHUNKS:
+                    project("kv", before_c - LAG, before_r)
+            if r == 0 and c + 1 < CHUNKS:
+                prepare_logit_weights(c + 1)
+            if r == 1 and 0 <= c + 1 - LAG < CHUNKS:
+                prepare_value_weights(c + 1 - LAG)
+            if t == logits_done:
+                shifted_logits()
+            if t == logits_done + 2:
+                exponentials()
+            if t == logits_done + 4:
+                denominators()
 
         nc.vector.tensor_tensor(
             out=products[:, :, 1:BLOCKS, 0:BLOCK_LEN],

@@ -23,16 +23,12 @@ FEATURES = 128
 BLOCK_LEN = 4
 TOKENS = SEQS * SEQ_LEN
 BLOCKS = SEQ_LEN // BLOCK_LEN
+WINDOWS = SEQS * BLOCKS
 WINDOW = 2 * BLOCK_LEN
 PASSES = D // K_PASS
 CHUNK_PASSES = 4
 CHUNKS = PASSES // CHUNK_PASSES
 CHUNK_K = CHUNK_PASSES * K_PASS
-ROUND_PASSES = 2
-CHUNK_ROUNDS = CHUNK_PASSES // ROUND_PASSES
-LAG = 4
-assert LAG >= 2
-ROUNDS = (CHUNKS + LAG) * CHUNK_ROUNDS
 WORDS_PASS = K_PASS // 2
 BANK_TOKENS = 2 * SEQ_LEN
 NEG = -3.4028234663852886e38
@@ -49,40 +45,11 @@ def tile_tokenlevelcompressor_pa_k_kernel(tc, h, w_kv_a, w_kv_b, w_z_a, w_z_b, b
         h_group = stack.enter_context(tc.tile_pool(name="h_group", bufs=4))
         w_in = stack.enter_context(tc.tile_pool(name="w_in", bufs=8))
         w_group = stack.enter_context(tc.tile_pool(name="w_group", bufs=4))
-        w_packed = stack.enter_context(tc.tile_pool(name="w_packed", bufs=8))
+        w_packed = stack.enter_context(tc.tile_pool(name="w_packed", bufs=4))
         soft = stack.enter_context(tc.tile_pool(name="soft", bufs=1))
         sums = stack.enter_context(tc.psum_pool(name="sums", bufs=1))
         banks = stack.enter_context(tc.psum_pool(name="banks", bufs=4))
         stack.enter_context(tc.manual_schedule())
-
-        def load_weight_chunk(weight, c):
-            w_raw = w_in.tile([P, CHUNK_PASSES, PACK * FEATURES], BF16)
-            rows = weight[c * CHUNK_K : (c + 1) * CHUNK_K, :]
-            nc.sync.dma_start(out=w_raw[:], in_=rows.rearrange("(g p t) n -> p g (t n)", p=P, t=PACK))
-            return w_raw
-
-        def regroup_on_vector(w_raw):
-            w_grouped = w_group.tile([P, CHUNK_PASSES, FEATURES, PACK], BF16, align_bytes=64)
-            nc.vector.tensor_copy(
-                out=w_grouped[:].rearrange("p g (c i) t -> p g c t i", i=4),
-                in_=w_raw[:].rearrange("p g (t c i) -> p g c t i", t=PACK, i=4),
-            )
-            return w_grouped
-
-        def regroup_on_scalar(w_raw):
-            w_grouped = w_group.tile([P, CHUNK_PASSES, FEATURES, PACK], BF16, align_bytes=64)
-            nc.scalar.copy(out=w_grouped[:], in_=w_raw[:].rearrange("p g (t n) -> p g n t", t=PACK))
-            return w_grouped
-
-        def quantise_weight_chunk(w_grouped):
-            w_codes = w_packed.tile([P, CHUNK_PASSES, FEATURES], U32, align_bytes=64)
-            w_scales = w_packed.tile([P, CHUNK_PASSES, FEATURES], U8, align_bytes=64)
-            nc.vector.quantize_mx(
-                out=w_codes[:].rearrange("p g n -> p (g n)").bitcast(FP8X4),
-                scales=w_scales[:].rearrange("p g n -> p (g n)"),
-                in_=w_grouped[:].rearrange("p g n t -> p (g n t)"),
-            )
-            return w_codes, w_scales
 
         ident = const.tile([P, P], F32)
         make_identity(nc, ident[:])
@@ -104,47 +71,19 @@ def tile_tokenlevelcompressor_pa_k_kernel(tc, h, w_kv_a, w_kv_b, w_z_a, w_z_b, b
         h_codes = keep.tile([P, PASSES, TOKENS], U32, align_bytes=64)
         h_scales = keep.tile([P, PASSES, TOKENS], U8, align_bytes=64)
 
-        z_a = sums.tile([P, TOKENS], F32)
-        z_b = sums.tile([P, TOKENS], F32)
-        c_a = sums.tile([P, TOKENS], F32)
-        c_b = sums.tile([P, TOKENS], F32)
+        def quantise_h_pass(g, h_grouped):
+            nc.vector.quantize_mx(
+                out=h_codes[:, g, :].bitcast(FP8X4),
+                scales=h_scales[:, g, :],
+                in_=h_grouped[:].rearrange("p n t -> p (n t)"),
+            )
 
         tokens_first = h.rearrange("b s d -> s b d")
-        h_raw_of = {}
-        raw_of = {}
-        packed_of = {}
-
-        def load_step(c):
-            if c < CHUNKS:
-                raw_of["z", c] = (load_weight_chunk(w_z_a, c), load_weight_chunk(w_z_b, c))
-            if 0 <= c - LAG < CHUNKS:
-                raw_of["kv", c - LAG] = (load_weight_chunk(w_kv_a, c - LAG), load_weight_chunk(w_kv_b, c - LAG))
-            if c < CHUNKS:
-                h_raw = h_in.tile([P, SEQS, CHUNK_K], BF16)
-                nc.sync.dma_start(out=h_raw[:], in_=tokens_first[:, :, c * CHUNK_K : (c + 1) * CHUNK_K])
-                h_raw_of[c] = h_raw
-
-        def prepare_logit_weights(c):
-            raw_a, raw_b = raw_of["z", c]
-            grouped_a = regroup_on_vector(raw_a)
-            grouped_b = regroup_on_vector(raw_b)
-            codes_a, scales_a = quantise_weight_chunk(grouped_a)
-            codes_b, scales_b = quantise_weight_chunk(grouped_b)
-            packed_of["z", c] = [(z_a, codes_a, scales_a), (z_b, codes_b, scales_b)]
-
-        def prepare_value_weights(c):
-            raw_a, raw_b = raw_of["kv", c]
-            grouped_b = regroup_on_scalar(raw_b)
-            grouped_a = regroup_on_vector(raw_a)
-            codes_a, scales_a = quantise_weight_chunk(grouped_a)
-            codes_b, scales_b = quantise_weight_chunk(grouped_b)
-            packed_of["kv", c] = [(c_b, codes_b, scales_b), (c_a, codes_a, scales_a)]
-
-        def quantise_h_round(c, r):
-            h_raw = h_raw_of[c]
-            local_passes = range(r * ROUND_PASSES, (r + 1) * ROUND_PASSES)
-            grouped_tiles = []
-            for gl in local_passes:
+        copied = None
+        for c in range(CHUNKS):
+            h_raw = h_in.tile([P, SEQS, CHUNK_K], BF16)
+            nc.sync.dma_start(out=h_raw[:], in_=tokens_first[:, :, c * CHUNK_K : (c + 1) * CHUNK_K])
+            for gl in range(CHUNK_PASSES):
                 h_grouped = h_group.tile([P, TOKENS, PACK], BF16, align_bytes=64)
                 grouped_words = (
                     h_grouped[:].rearrange("p n t -> p (n t)").bitcast(F32).rearrange("p (n u) -> p n u", u=2)
@@ -159,42 +98,35 @@ def tile_tokenlevelcompressor_pa_k_kernel(tc, h, w_kv_a, w_kv_b, w_z_a, w_z_b, b
                                 words[:, gl * WORDS_PASS + u : (gl + 1) * WORDS_PASS : 2],
                                 ident[:],
                             )
-                    nc.scalar.copy(
-                        out=grouped_words[:, half * BANK_TOKENS : (half + 1) * BANK_TOKENS, :],
-                        in_=bank[:].rearrange("p u n -> p n u"),
-                    )
-                grouped_tiles.append(h_grouped)
-            for gl, h_grouped in zip(local_passes, grouped_tiles):
-                g = c * CHUNK_PASSES + gl
-                nc.vector.quantize_mx(
-                    out=h_codes[:, g, :].bitcast(FP8X4),
-                    scales=h_scales[:, g, :],
-                    in_=h_grouped[:].rearrange("p n t -> p (n t)"),
-                )
+                    grouped_half = grouped_words[:, half * BANK_TOKENS : (half + 1) * BANK_TOKENS, :]
+                    if gl % 2 == 1 and half == 1:
+                        nc.vector.tensor_copy(out=grouped_half, in_=bank[:].rearrange("p u n -> p n u"))
+                    else:
+                        nc.scalar.copy(out=grouped_half, in_=bank[:].rearrange("p u n -> p n u"))
+                if copied is not None:
+                    quantise_h_pass(copied[0], copied[1])
+                copied = (c * CHUNK_PASSES + gl, h_grouped)
+        quantise_h_pass(copied[0], copied[1])
 
-        def project(kind, c, r):
-            for acc, w_codes, w_scales in packed_of[kind, c]:
-                for gl in range(r * ROUND_PASSES, (r + 1) * ROUND_PASSES):
-                    g = c * CHUNK_PASSES + gl
-                    nc.tensor.matmul_mx(
-                        out=acc[:],
-                        lhsT=w_codes[:, gl, :].bitcast(FP8X4),
-                        lhsT_scale=w_scales[:, gl, :],
-                        rhs=h_codes[:, g, :].bitcast(FP8X4),
-                        rhs_scale=h_scales[:, g, :],
-                        start=(g == 0),
-                        stop=(g == PASSES - 1),
-                    )
+        bias_rows_f32 = const.tile([P, FEATURES], F32)
+        nc.vector.tensor_copy(out=bias_rows_f32[:], in_=bias_rows[:])
+        bias_bank = banks.tile([P, 2, BANK_TOKENS], F32, name="bank")
+        nc.tensor.transpose(bias_bank[:, 0, 0:P], bias_rows_f32[:], ident[:])
+        bias = const.tile([P, WINDOW], F32)
 
+        z_a = sums.tile([P, TOKENS], F32)
+        z_b = sums.tile([P, TOKENS], F32)
+        c_a = sums.tile([P, TOKENS], F32)
+        c_b = sums.tile([P, TOKENS], F32)
         by_block = "p (b j i) -> p b j i"
         windows = logits[:].rearrange("p b j s -> p (b j) s")
-        bias = const.tile([P, WINDOW], F32)
-        top = soft.tile([P, SEQS * BLOCKS], F32)
+        top = soft.tile([P, WINDOWS], F32)
         expd = soft.tile([P, SEQS, BLOCKS, WINDOW], F32)
-        denom = soft.tile([P, SEQS * BLOCKS], F32)
-        inv_denom = soft.tile([P, SEQS * BLOCKS], F32)
+        denom = soft.tile([P, WINDOWS], F32)
+        inv_denom = soft.tile([P, WINDOWS], F32)
 
         def shifted_logits():
+            nc.vector.tensor_copy(out=bias[:], in_=bias_bank[:, 0, 0:WINDOW])
             nc.vector.tensor_tensor(
                 out=logits[:, :, 1:BLOCKS, 0:BLOCK_LEN],
                 in0=z_b[:].rearrange(by_block, b=SEQS, i=BLOCK_LEN)[:, :, 0 : BLOCKS - 1, :],
@@ -211,7 +143,7 @@ def tile_tokenlevelcompressor_pa_k_kernel(tc, h, w_kv_a, w_kv_b, w_z_a, w_z_b, b
             nc.vector.tensor_tensor(
                 out=windows,
                 in0=windows,
-                in1=top[:].unsqueeze(2).to_broadcast([P, SEQS * BLOCKS, WINDOW]),
+                in1=top[:].unsqueeze(2).to_broadcast([P, WINDOWS, WINDOW]),
                 op=ALU.subtract,
             )
 
@@ -224,56 +156,97 @@ def tile_tokenlevelcompressor_pa_k_kernel(tc, h, w_kv_a, w_kv_b, w_z_a, w_z_b, b
             )
             nc.vector.reciprocal(out=inv_denom[:], in_=denom[:])
 
-        load_step(0)
-        prepare_logit_weights(0)
+        def previous_block_products():
+            nc.vector.tensor_tensor(
+                out=products[:, :, 1:BLOCKS, 0:BLOCK_LEN],
+                in0=c_b[:].rearrange(by_block, b=SEQS, i=BLOCK_LEN)[:, :, 0 : BLOCKS - 1, :],
+                in1=expd[:, :, 1:BLOCKS, 0:BLOCK_LEN],
+                op=ALU.mult,
+            )
 
-        bias_rows_f32 = const.tile([P, FEATURES], F32)
-        nc.vector.tensor_copy(out=bias_rows_f32[:], in_=bias_rows[:])
-        bias_bank = banks.tile([P, 2, BANK_TOKENS], F32, name="bank")
-        nc.tensor.transpose(bias_bank[:, 0, 0:P], bias_rows_f32[:], ident[:])
-        nc.vector.tensor_copy(out=bias[:], in_=bias_bank[:, 0, 0:WINDOW])
+        pieces = []
+        for c in range(CHUNKS):
+            pieces.append((z_a, w_z_a, c))
+            pieces.append((z_b, w_z_b, c))
+        for c in range(CHUNKS):
+            pieces.append((c_b, w_kv_b, c))
+        for c in range(CHUNKS):
+            pieces.append((c_a, w_kv_a, c))
+        logits_done = 2 * CHUNKS + 2
+        values_b_done = 3 * CHUNKS + 2
 
-        logits_done = CHUNKS * CHUNK_ROUNDS
-        for t in range(ROUNDS + 1):
-            c, r = divmod(t, CHUNK_ROUNDS)
-            if r == 0:
-                load_step(c + 1)
-            if c < CHUNKS:
-                quantise_h_round(c, r)
-            if t >= 1:
-                before_c, before_r = divmod(t - 1, CHUNK_ROUNDS)
-                if before_c < CHUNKS:
-                    project("z", before_c, before_r)
-                if 0 <= before_c - LAG < CHUNKS:
-                    project("kv", before_c - LAG, before_r)
-            if r == 0 and c + 1 < CHUNKS:
-                prepare_logit_weights(c + 1)
-            if r == 1 and 0 <= c + 1 - LAG < CHUNKS:
-                prepare_value_weights(c + 1 - LAG)
-            if t == logits_done:
+        def regroup(i):
+            weight, c = pieces[i][1], pieces[i][2]
+            w_raw = w_in.tile([P, CHUNK_PASSES, PACK * FEATURES], BF16)
+            rows = weight[c * CHUNK_K : (c + 1) * CHUNK_K, :]
+            nc.sync.dma_start(out=w_raw[:], in_=rows.rearrange("(g p t) n -> p g (t n)", p=P, t=PACK))
+            w_grouped = w_group.tile([P, CHUNK_PASSES, FEATURES, PACK], BF16, align_bytes=64)
+            if i % 2 == 1:
+                nc.vector.tensor_copy(
+                    out=w_grouped[:].rearrange("p g (c i) t -> p g c t i", i=4),
+                    in_=w_raw[:].rearrange("p g (t c i) -> p g c t i", t=PACK, i=4),
+                )
+            else:
+                for gl in range(CHUNK_PASSES):
+                    nc.scalar.copy(
+                        out=w_grouped[:, gl].rearrange("p (c i) t -> p c t i", i=4),
+                        in_=w_raw[:, gl].rearrange("p (t c i) -> p c t i", t=PACK, i=4),
+                    )
+            return w_grouped
+
+        def quantise(w_grouped):
+            w_codes = w_packed.tile([P, CHUNK_PASSES, FEATURES], U32, align_bytes=64)
+            w_scales = w_packed.tile([P, CHUNK_PASSES, FEATURES], U8, align_bytes=64)
+            nc.vector.quantize_mx(
+                out=w_codes[:].rearrange("p g n -> p (g n)").bitcast(FP8X4),
+                scales=w_scales[:].rearrange("p g n -> p (g n)"),
+                in_=w_grouped[:].rearrange("p g n t -> p (g n t)"),
+            )
+            return w_codes, w_scales
+
+        def project(i, w_codes, w_scales):
+            acc, c = pieces[i][0], pieces[i][2]
+            for gl in range(CHUNK_PASSES):
+                g = c * CHUNK_PASSES + gl
+                nc.tensor.matmul_mx(
+                    out=acc[:],
+                    lhsT=w_codes[:, gl, :].bitcast(FP8X4),
+                    lhsT_scale=w_scales[:, gl, :],
+                    rhs=h_codes[:, g, :].bitcast(FP8X4),
+                    rhs_scale=h_scales[:, g, :],
+                    start=(g == 0),
+                    stop=(g == PASSES - 1),
+                )
+
+        grouped_of = {}
+        packed_of = {}
+        for i in range(len(pieces) + 2):
+            if i < len(pieces):
+                grouped_of[i] = regroup(i)
+            if 1 <= i <= len(pieces):
+                packed_of[i - 1] = quantise(grouped_of[i - 1])
+            if i >= 2:
+                project(i - 2, packed_of[i - 2][0], packed_of[i - 2][1])
+            if i == logits_done:
                 shifted_logits()
-            if t == logits_done + 2:
+            if i == logits_done + 2:
                 exponentials()
-            if t == logits_done + 4:
+            if i == logits_done + 6:
                 denominators()
+            if i == values_b_done:
+                previous_block_products()
 
-        nc.vector.tensor_tensor(
-            out=products[:, :, 1:BLOCKS, 0:BLOCK_LEN],
-            in0=c_b[:].rearrange(by_block, b=SEQS, i=BLOCK_LEN)[:, :, 0 : BLOCKS - 1, :],
-            in1=expd[:, :, 1:BLOCKS, 0:BLOCK_LEN],
-            op=ALU.mult,
-        )
         nc.vector.tensor_tensor(
             out=products[:, :, :, BLOCK_LEN:WINDOW],
             in0=c_a[:].rearrange(by_block, b=SEQS, i=BLOCK_LEN),
             in1=expd[:, :, :, BLOCK_LEN:WINDOW],
             op=ALU.mult,
         )
-        numer = soft.tile([P, SEQS * BLOCKS], F32)
+        numer = soft.tile([P, WINDOWS], F32)
         nc.vector.tensor_reduce(
             out=numer[:], in_=products[:].rearrange("p b j s -> p (b j) s"), axis=AXIS.X, op=ALU.add
         )
-        result = soft.tile([P, SEQS * BLOCKS], F32)
+        result = soft.tile([P, WINDOWS], F32)
         nc.vector.tensor_tensor(out=result[:], in0=numer[:], in1=inv_denom[:], op=ALU.mult)
 
         result_bank = banks.tile([P, 2, BANK_TOKENS], F32, name="bank")

@@ -30,7 +30,9 @@ CHUNK_PASSES = 4
 CHUNKS = PASSES // CHUNK_PASSES
 CHUNK_K = CHUNK_PASSES * K_PASS
 WORDS_PASS = K_PASS // 2
-BANK_TOKENS = 2 * SEQ_LEN
+TILE_PASSES = 8
+BANK_PASSES = 2
+TILE_BANKS = TILE_PASSES // BANK_PASSES
 NEG = -3.4028234663852886e38
 
 FLOPS = 2 * TOKENS * D * 4 * FEATURES
@@ -41,8 +43,8 @@ def tile_tokenlevelcompressor_pa_k_kernel(tc, h, w_kv_a, w_kv_b, w_z_a, w_z_b, b
     with ExitStack() as stack:
         const = stack.enter_context(tc.tile_pool(name="const", bufs=1))
         keep = stack.enter_context(tc.tile_pool(name="keep", bufs=1))
-        h_in = stack.enter_context(tc.tile_pool(name="h_in", bufs=3))
-        h_group = stack.enter_context(tc.tile_pool(name="h_group", bufs=4))
+        h_in = stack.enter_context(tc.tile_pool(name="h_in", bufs=6))
+        h_group = stack.enter_context(tc.tile_pool(name="h_group", bufs=6))
         w_in = stack.enter_context(tc.tile_pool(name="w_in", bufs=8))
         w_group = stack.enter_context(tc.tile_pool(name="w_group", bufs=4))
         w_packed = stack.enter_context(tc.tile_pool(name="w_packed", bufs=4))
@@ -71,47 +73,53 @@ def tile_tokenlevelcompressor_pa_k_kernel(tc, h, w_kv_a, w_kv_b, w_z_a, w_z_b, b
         h_codes = keep.tile([P, PASSES, TOKENS], U32, align_bytes=64)
         h_scales = keep.tile([P, PASSES, TOKENS], U8, align_bytes=64)
 
-        def quantise_h_pass(g, h_grouped):
-            nc.vector.quantize_mx(
-                out=h_codes[:, g, :].bitcast(FP8X4),
-                scales=h_scales[:, g, :],
-                in_=h_grouped[:].rearrange("p n t -> p (n t)"),
-            )
-
-        tokens_first = h.rearrange("b s d -> s b d")
-        copied = None
-        for c in range(CHUNKS):
-            h_raw = h_in.tile([P, SEQS, CHUNK_K], BF16)
-            nc.sync.dma_start(out=h_raw[:], in_=tokens_first[:, :, c * CHUNK_K : (c + 1) * CHUNK_K])
-            for gl in range(CHUNK_PASSES):
-                h_grouped = h_group.tile([P, TOKENS, PACK], BF16, align_bytes=64)
-                grouped_words = (
-                    h_grouped[:].rearrange("p n t -> p (n t)").bitcast(F32).rearrange("p (n u) -> p n u", u=2)
+        def quantise_h_bank(b, first, h_grouped):
+            tokens = slice(b * SEQ_LEN, (b + 1) * SEQ_LEN)
+            for q in range(BANK_PASSES):
+                nc.vector.quantize_mx(
+                    out=h_codes[:, first + q, tokens].bitcast(FP8X4),
+                    scales=h_scales[:, first + q, tokens],
+                    in_=h_grouped[:, q].rearrange("p n t -> p (n t)"),
                 )
-                for half in range(TOKENS // BANK_TOKENS):
-                    bank = banks.tile([P, 2, BANK_TOKENS], F32)
-                    for u in range(2):
-                        for s in range(2):
-                            words = h_raw[:, 2 * half + s, :].bitcast(F32)
+
+        copied = None
+        for b in range(SEQS):
+            for tile_first in range(0, PASSES, TILE_PASSES):
+                h_raw = h_in.tile([P, TILE_PASSES * K_PASS], BF16)
+                nc.sync.dma_start(
+                    out=h_raw[:], in_=h[b, :, tile_first * K_PASS : (tile_first + TILE_PASSES) * K_PASS]
+                )
+                words = h_raw[:].bitcast(F32)
+                for bank_no in range(TILE_BANKS):
+                    bank = banks.tile([P, BANK_PASSES, 2, SEQ_LEN], F32)
+                    for q in range(BANK_PASSES):
+                        gl = bank_no * BANK_PASSES + q
+                        for u in range(2):
                             nc.tensor.transpose(
-                                bank[:, u, s * SEQ_LEN : (s + 1) * SEQ_LEN],
+                                bank[:, q, u, :],
                                 words[:, gl * WORDS_PASS + u : (gl + 1) * WORDS_PASS : 2],
                                 ident[:],
                             )
-                    grouped_half = grouped_words[:, half * BANK_TOKENS : (half + 1) * BANK_TOKENS, :]
-                    if gl % 2 == 1 and half == 1:
-                        nc.vector.tensor_copy(out=grouped_half, in_=bank[:].rearrange("p u n -> p n u"))
+                    h_grouped = h_group.tile([P, BANK_PASSES, SEQ_LEN, PACK], BF16, align_bytes=64)
+                    grouped_words = (
+                        h_grouped[:]
+                        .rearrange("p q n t -> p (q n t)")
+                        .bitcast(F32)
+                        .rearrange("p (q n u) -> p q n u", q=BANK_PASSES, u=2)
+                    )
+                    if bank_no == TILE_BANKS - 1:
+                        nc.vector.tensor_copy(out=grouped_words, in_=bank[:].rearrange("p q u n -> p q n u"))
                     else:
-                        nc.scalar.copy(out=grouped_half, in_=bank[:].rearrange("p u n -> p n u"))
-                if copied is not None:
-                    quantise_h_pass(copied[0], copied[1])
-                copied = (c * CHUNK_PASSES + gl, h_grouped)
-        quantise_h_pass(copied[0], copied[1])
+                        nc.scalar.copy(out=grouped_words, in_=bank[:].rearrange("p q u n -> p q n u"))
+                    if copied is not None:
+                        quantise_h_bank(*copied)
+                    copied = (b, tile_first + bank_no * BANK_PASSES, h_grouped)
+        quantise_h_bank(*copied)
 
         bias_rows_f32 = const.tile([P, FEATURES], F32)
         nc.vector.tensor_copy(out=bias_rows_f32[:], in_=bias_rows[:])
-        bias_bank = banks.tile([P, 2, BANK_TOKENS], F32, name="bank")
-        nc.tensor.transpose(bias_bank[:, 0, 0:P], bias_rows_f32[:], ident[:])
+        bias_bank = banks.tile([P, BANK_PASSES, 2, SEQ_LEN], F32, name="bank")
+        nc.tensor.transpose(bias_bank[:, 0, 0, :], bias_rows_f32[:], ident[:])
         bias = const.tile([P, WINDOW], F32)
 
         z_a = sums.tile([P, TOKENS], F32)
@@ -126,7 +134,7 @@ def tile_tokenlevelcompressor_pa_k_kernel(tc, h, w_kv_a, w_kv_b, w_z_a, w_z_b, b
         inv_denom = soft.tile([P, WINDOWS], F32)
 
         def shifted_logits():
-            nc.vector.tensor_copy(out=bias[:], in_=bias_bank[:, 0, 0:WINDOW])
+            nc.vector.tensor_copy(out=bias[:], in_=bias_bank[:, 0, 0, 0:WINDOW])
             nc.vector.tensor_tensor(
                 out=logits[:, :, 1:BLOCKS, 0:BLOCK_LEN],
                 in0=z_b[:].rearrange(by_block, b=SEQS, i=BLOCK_LEN)[:, :, 0 : BLOCKS - 1, :],
@@ -181,17 +189,17 @@ def tile_tokenlevelcompressor_pa_k_kernel(tc, h, w_kv_a, w_kv_b, w_z_a, w_z_b, b
             rows = weight[c * CHUNK_K : (c + 1) * CHUNK_K, :]
             nc.sync.dma_start(out=w_raw[:], in_=rows.rearrange("(g p t) n -> p g (t n)", p=P, t=PACK))
             w_grouped = w_group.tile([P, CHUNK_PASSES, FEATURES, PACK], BF16, align_bytes=64)
-            if i % 2 == 1:
-                nc.vector.tensor_copy(
-                    out=w_grouped[:].rearrange("p g (c i) t -> p g c t i", i=4),
-                    in_=w_raw[:].rearrange("p g (t c i) -> p g c t i", t=PACK, i=4),
-                )
-            else:
+            if i % 2 == 0 or (i >= 2 * CHUNKS and i % 8 == 3):
                 for gl in range(CHUNK_PASSES):
                     nc.scalar.copy(
                         out=w_grouped[:, gl].rearrange("p (c i) t -> p c t i", i=4),
                         in_=w_raw[:, gl].rearrange("p (t c i) -> p c t i", t=PACK, i=4),
                     )
+            else:
+                nc.vector.tensor_copy(
+                    out=w_grouped[:].rearrange("p g (c i) t -> p g c t i", i=4),
+                    in_=w_raw[:].rearrange("p g (t c i) -> p g c t i", t=PACK, i=4),
+                )
             return w_grouped
 
         def quantise(w_grouped):
@@ -249,8 +257,8 @@ def tile_tokenlevelcompressor_pa_k_kernel(tc, h, w_kv_a, w_kv_b, w_z_a, w_z_b, b
         result = soft.tile([P, WINDOWS], F32)
         nc.vector.tensor_tensor(out=result[:], in0=numer[:], in1=inv_denom[:], op=ALU.mult)
 
-        result_bank = banks.tile([P, 2, BANK_TOKENS], F32, name="bank")
-        nc.tensor.transpose(result_bank[:, 0, 0:P], result[:], ident[:])
+        result_bank = banks.tile([P, BANK_PASSES, 2, SEQ_LEN], F32, name="bank")
+        nc.tensor.transpose(result_bank[:, 0, 0, :], result[:], ident[:])
         rows_out = soft.tile([P, FEATURES], F32)
-        nc.vector.tensor_copy(out=rows_out[:], in_=result_bank[:, 0, 0:P])
+        nc.vector.tensor_copy(out=rows_out[:], in_=result_bank[:, 0, 0, :])
         nc.sync.dma_start(out=out.rearrange("b j f -> (b j) f"), in_=rows_out[:])

@@ -33,6 +33,7 @@ WORDS_PASS = K_PASS // 2
 TILE_PASSES = 8
 BANK_PASSES = 2
 TILE_BANKS = TILE_PASSES // BANK_PASSES
+VECTOR_BANK = 8
 NEG = -3.4028234663852886e38
 
 FLOPS = 2 * TOKENS * D * 4 * FEATURES
@@ -66,9 +67,10 @@ def tile_tokenlevelcompressor_pa_k_kernel(tc, h, w_kv_a, w_kv_b, w_z_a, w_z_b, b
         nc.scalar.activation(out=warm[:], in_=warm[:], func=ACT.Exp)
 
         logits = soft.tile([P, SEQS, BLOCKS, WINDOW], F32)
-        products = soft.tile([P, SEQS, BLOCKS, WINDOW], F32)
+        products_b = soft.tile([P, SEQS, BLOCKS, BLOCK_LEN], F32)
+        products_a = soft.tile([P, SEQS, BLOCKS, BLOCK_LEN], F32)
         nc.vector.memset(logits[:, :, 0:1, 0:BLOCK_LEN], NEG)
-        nc.vector.memset(products[:, :, 0:1, 0:BLOCK_LEN], 0.0)
+        nc.vector.memset(products_b[:, :, 0:1, :], 0.0)
 
         h_codes = keep.tile([P, PASSES, TOKENS], U32, align_bytes=64)
         h_scales = keep.tile([P, PASSES, TOKENS], U8, align_bytes=64)
@@ -107,7 +109,7 @@ def tile_tokenlevelcompressor_pa_k_kernel(tc, h, w_kv_a, w_kv_b, w_z_a, w_z_b, b
                         .bitcast(F32)
                         .rearrange("p (q n u) -> p q n u", q=BANK_PASSES, u=2)
                     )
-                    if bank_no == TILE_BANKS - 1:
+                    if (tile_first // BANK_PASSES + bank_no) % VECTOR_BANK == VECTOR_BANK - 1:
                         nc.vector.tensor_copy(out=grouped_words, in_=bank[:].rearrange("p q u n -> p q n u"))
                     else:
                         nc.scalar.copy(out=grouped_words, in_=bank[:].rearrange("p q u n -> p q n u"))
@@ -131,7 +133,7 @@ def tile_tokenlevelcompressor_pa_k_kernel(tc, h, w_kv_a, w_kv_b, w_z_a, w_z_b, b
         top = soft.tile([P, WINDOWS], F32)
         expd = soft.tile([P, SEQS, BLOCKS, WINDOW], F32)
         denom = soft.tile([P, WINDOWS], F32)
-        inv_denom = soft.tile([P, WINDOWS], F32)
+        inv_denom = soft.tile([P, FEATURES], F32)
 
         def shifted_logits():
             nc.vector.tensor_copy(out=bias[:], in_=bias_bank[:, 0, 0, 0:WINDOW])
@@ -162,11 +164,13 @@ def tile_tokenlevelcompressor_pa_k_kernel(tc, h, w_kv_a, w_kv_b, w_z_a, w_z_b, b
             nc.vector.tensor_reduce(
                 out=denom[:], in_=expd[:].rearrange("p b j s -> p (b j) s"), axis=AXIS.X, op=ALU.add
             )
-            nc.vector.reciprocal(out=inv_denom[:], in_=denom[:])
+
+        def inverses():
+            nc.vector.reciprocal(out=inv_denom[:], in_=denom_bank[:, 0, 0, :])
 
         def previous_block_products():
             nc.vector.tensor_tensor(
-                out=products[:, :, 1:BLOCKS, 0:BLOCK_LEN],
+                out=products_b[:, :, 1:BLOCKS, :],
                 in0=c_b[:].rearrange(by_block, b=SEQS, i=BLOCK_LEN)[:, :, 0 : BLOCKS - 1, :],
                 in1=expd[:, :, 1:BLOCKS, 0:BLOCK_LEN],
                 op=ALU.mult,
@@ -174,48 +178,51 @@ def tile_tokenlevelcompressor_pa_k_kernel(tc, h, w_kv_a, w_kv_b, w_z_a, w_z_b, b
 
         pieces = []
         for c in range(CHUNKS):
-            pieces.append((z_a, w_z_a, c))
-            pieces.append((z_b, w_z_b, c))
+            pieces.append((z_a, w_z_a, c * CHUNK_PASSES, CHUNK_PASSES))
+            pieces.append((z_b, w_z_b, c * CHUNK_PASSES, CHUNK_PASSES))
         for c in range(CHUNKS):
-            pieces.append((c_b, w_kv_b, c))
-        for c in range(CHUNKS):
-            pieces.append((c_a, w_kv_a, c))
+            pieces.append((c_b, w_kv_b, c * CHUNK_PASSES, CHUNK_PASSES))
+        for c in range(CHUNKS - 1):
+            pieces.append((c_a, w_kv_a, c * CHUNK_PASSES, CHUNK_PASSES))
+        for first in range(PASSES - CHUNK_PASSES, PASSES, CHUNK_PASSES // 2):
+            pieces.append((c_a, w_kv_a, first, CHUNK_PASSES // 2))
         logits_done = 2 * CHUNKS + 2
         values_b_done = 3 * CHUNKS + 2
 
         def regroup(i):
-            weight, c = pieces[i][1], pieces[i][2]
+            acc, weight, first, count = pieces[i]
             w_raw = w_in.tile([P, CHUNK_PASSES, PACK * FEATURES], BF16)
-            rows = weight[c * CHUNK_K : (c + 1) * CHUNK_K, :]
-            nc.sync.dma_start(out=w_raw[:], in_=rows.rearrange("(g p t) n -> p g (t n)", p=P, t=PACK))
+            rows = weight[first * K_PASS : (first + count) * K_PASS, :]
+            nc.sync.dma_start(out=w_raw[:, 0:count], in_=rows.rearrange("(g p t) n -> p g (t n)", p=P, t=PACK))
             w_grouped = w_group.tile([P, CHUNK_PASSES, FEATURES, PACK], BF16, align_bytes=64)
-            if i % 2 == 0 or (i >= 2 * CHUNKS and i % 8 == 3):
-                for gl in range(CHUNK_PASSES):
+            if (i % 2 == 0 and i < len(pieces) - 2) or (i >= 2 * CHUNKS and i % 8 == 3) or i == len(pieces) - 2:
+                for gl in range(count):
                     nc.scalar.copy(
                         out=w_grouped[:, gl].rearrange("p (c i) t -> p c t i", i=4),
                         in_=w_raw[:, gl].rearrange("p (t c i) -> p c t i", t=PACK, i=4),
                     )
             else:
                 nc.vector.tensor_copy(
-                    out=w_grouped[:].rearrange("p g (c i) t -> p g c t i", i=4),
-                    in_=w_raw[:].rearrange("p g (t c i) -> p g c t i", t=PACK, i=4),
+                    out=w_grouped[:, 0:count].rearrange("p g (c i) t -> p g c t i", i=4),
+                    in_=w_raw[:, 0:count].rearrange("p g (t c i) -> p g c t i", t=PACK, i=4),
                 )
             return w_grouped
 
-        def quantise(w_grouped):
+        def quantise(i, w_grouped):
+            count = pieces[i][3]
             w_codes = w_packed.tile([P, CHUNK_PASSES, FEATURES], U32, align_bytes=64)
             w_scales = w_packed.tile([P, CHUNK_PASSES, FEATURES], U8, align_bytes=64)
             nc.vector.quantize_mx(
-                out=w_codes[:].rearrange("p g n -> p (g n)").bitcast(FP8X4),
-                scales=w_scales[:].rearrange("p g n -> p (g n)"),
-                in_=w_grouped[:].rearrange("p g n t -> p (g n t)"),
+                out=w_codes[:, 0:count].rearrange("p g n -> p (g n)").bitcast(FP8X4),
+                scales=w_scales[:, 0:count].rearrange("p g n -> p (g n)"),
+                in_=w_grouped[:, 0:count].rearrange("p g n t -> p (g n t)"),
             )
             return w_codes, w_scales
 
         def project(i, w_codes, w_scales):
-            acc, c = pieces[i][0], pieces[i][2]
-            for gl in range(CHUNK_PASSES):
-                g = c * CHUNK_PASSES + gl
+            acc, weight, first, count = pieces[i]
+            for gl in range(count):
+                g = first + gl
                 nc.tensor.matmul_mx(
                     out=acc[:],
                     lhsT=w_codes[:, gl, :].bitcast(FP8X4),
@@ -232,7 +239,7 @@ def tile_tokenlevelcompressor_pa_k_kernel(tc, h, w_kv_a, w_kv_b, w_z_a, w_z_b, b
             if i < len(pieces):
                 grouped_of[i] = regroup(i)
             if 1 <= i <= len(pieces):
-                packed_of[i - 1] = quantise(grouped_of[i - 1])
+                packed_of[i - 1] = quantise(i - 1, grouped_of[i - 1])
             if i >= 2:
                 project(i - 2, packed_of[i - 2][0], packed_of[i - 2][1])
             if i == logits_done:
@@ -241,24 +248,33 @@ def tile_tokenlevelcompressor_pa_k_kernel(tc, h, w_kv_a, w_kv_b, w_z_a, w_z_b, b
                 exponentials()
             if i == logits_done + 6:
                 denominators()
+            if i == logits_done + 7:
+                denom_bank = banks.tile([P, BANK_PASSES, 2, SEQ_LEN], F32, name="bank")
+                nc.tensor.transpose(denom_bank[:, 0, 0, :], denom[:], ident[:])
+            if i == logits_done + 10:
+                inverses()
             if i == values_b_done:
                 previous_block_products()
 
+        sum_b = soft.tile([P, WINDOWS], F32)
+        nc.vector.tensor_reduce(
+            out=sum_b[:], in_=products_b[:].rearrange("p b j i -> p (b j) i"), axis=AXIS.X, op=ALU.add
+        )
         nc.vector.tensor_tensor(
-            out=products[:, :, :, BLOCK_LEN:WINDOW],
+            out=products_a[:],
             in0=c_a[:].rearrange(by_block, b=SEQS, i=BLOCK_LEN),
             in1=expd[:, :, :, BLOCK_LEN:WINDOW],
             op=ALU.mult,
         )
-        numer = soft.tile([P, WINDOWS], F32)
+        sum_a = soft.tile([P, WINDOWS], F32)
         nc.vector.tensor_reduce(
-            out=numer[:], in_=products[:].rearrange("p b j s -> p (b j) s"), axis=AXIS.X, op=ALU.add
+            out=sum_a[:], in_=products_a[:].rearrange("p b j i -> p (b j) i"), axis=AXIS.X, op=ALU.add
         )
-        result = soft.tile([P, WINDOWS], F32)
-        nc.vector.tensor_tensor(out=result[:], in0=numer[:], in1=inv_denom[:], op=ALU.mult)
+        numer = soft.tile([P, WINDOWS], F32)
+        nc.vector.tensor_tensor(out=numer[:], in0=sum_a[:], in1=sum_b[:], op=ALU.add)
 
         result_bank = banks.tile([P, BANK_PASSES, 2, SEQ_LEN], F32, name="bank")
-        nc.tensor.transpose(result_bank[:, 0, 0, :], result[:], ident[:])
+        nc.tensor.transpose(result_bank[:, 0, 0, :], numer[:], ident[:])
         rows_out = soft.tile([P, FEATURES], F32)
-        nc.vector.tensor_copy(out=rows_out[:], in_=result_bank[:, 0, 0, :])
+        nc.vector.tensor_tensor(out=rows_out[:], in0=result_bank[:, 0, 0, :], in1=inv_denom[:], op=ALU.mult)
         nc.sync.dma_start(out=out.rearrange("b j f -> (b j) f"), in_=rows_out[:])

@@ -47,7 +47,7 @@ def tile_tokenlevelcompressor_pa_k_kernel(tc, h, w_kv_a, w_kv_b, w_z_a, w_z_b, b
         h_in = stack.enter_context(tc.tile_pool(name="h_in", bufs=6))
         h_group = stack.enter_context(tc.tile_pool(name="h_group", bufs=6))
         w_in = stack.enter_context(tc.tile_pool(name="w_in", bufs=8))
-        w_group = stack.enter_context(tc.tile_pool(name="w_group", bufs=4))
+        w_group = stack.enter_context(tc.tile_pool(name="w_group", bufs=6))
         w_packed = stack.enter_context(tc.tile_pool(name="w_packed", bufs=4))
         soft = stack.enter_context(tc.tile_pool(name="soft", bufs=1))
         sums = stack.enter_context(tc.psum_pool(name="sums", bufs=1))
@@ -135,21 +135,26 @@ def tile_tokenlevelcompressor_pa_k_kernel(tc, h, w_kv_a, w_kv_b, w_z_a, w_z_b, b
         denom = soft.tile([P, WINDOWS], F32)
         inv_denom = soft.tile([P, FEATURES], F32)
 
-        def shifted_logits():
-            nc.vector.tensor_copy(out=bias[:], in_=bias_bank[:, 0, 0, 0:WINDOW])
+        def previous_block_logits():
             nc.vector.tensor_tensor(
                 out=logits[:, :, 1:BLOCKS, 0:BLOCK_LEN],
                 in0=z_b[:].rearrange(by_block, b=SEQS, i=BLOCK_LEN)[:, :, 0 : BLOCKS - 1, :],
                 in1=bias[:, 0:BLOCK_LEN].unsqueeze(1).unsqueeze(1).to_broadcast([P, SEQS, BLOCKS - 1, BLOCK_LEN]),
                 op=ALU.add,
             )
+
+        def own_block_logits():
             nc.vector.tensor_tensor(
                 out=logits[:, :, :, BLOCK_LEN:WINDOW],
                 in0=z_a[:].rearrange(by_block, b=SEQS, i=BLOCK_LEN),
                 in1=bias[:, BLOCK_LEN:WINDOW].unsqueeze(1).unsqueeze(1).to_broadcast([P, SEQS, BLOCKS, BLOCK_LEN]),
                 op=ALU.add,
             )
+
+        def largest():
             nc.vector.tensor_reduce(out=top[:], in_=windows, axis=AXIS.X, op=ALU.max)
+
+        def shifted_logits():
             nc.vector.tensor_tensor(
                 out=windows,
                 in0=windows,
@@ -195,7 +200,7 @@ def tile_tokenlevelcompressor_pa_k_kernel(tc, h, w_kv_a, w_kv_b, w_z_a, w_z_b, b
             rows = weight[first * K_PASS : (first + count) * K_PASS, :]
             nc.sync.dma_start(out=w_raw[:, 0:count], in_=rows.rearrange("(g p t) n -> p g (t n)", p=P, t=PACK))
             w_grouped = w_group.tile([P, CHUNK_PASSES, FEATURES, PACK], BF16, align_bytes=64)
-            if (i % 2 == 0 and i < len(pieces) - 2) or (i >= 2 * CHUNKS and i % 8 == 3) or i == len(pieces) - 2:
+            if (i % 2 == 0 and i < len(pieces) - 2) or (i >= 2 * CHUNKS and i % 16 == 3) or i == len(pieces) - 2:
                 for gl in range(count):
                     nc.scalar.copy(
                         out=w_grouped[:, gl].rearrange("p (c i) t -> p c t i", i=4),
@@ -243,15 +248,22 @@ def tile_tokenlevelcompressor_pa_k_kernel(tc, h, w_kv_a, w_kv_b, w_z_a, w_z_b, b
             if i >= 2:
                 project(i - 2, packed_of[i - 2][0], packed_of[i - 2][1])
             if i == logits_done:
-                shifted_logits()
+                nc.vector.tensor_copy(out=bias[:], in_=bias_bank[:, 0, 0, 0:WINDOW])
+                own_block_logits()
+            if i == logits_done + 1:
+                previous_block_logits()
             if i == logits_done + 2:
+                largest()
+            if i == logits_done + 3:
+                shifted_logits()
+            if i == logits_done + 5:
                 exponentials()
-            if i == logits_done + 6:
+            if i == logits_done + 8:
                 denominators()
-            if i == logits_done + 7:
+            if i == logits_done + 9:
                 denom_bank = banks.tile([P, BANK_PASSES, 2, SEQ_LEN], F32, name="bank")
                 nc.tensor.transpose(denom_bank[:, 0, 0, :], denom[:], ident[:])
-            if i == logits_done + 10:
+            if i == logits_done + 12:
                 inverses()
             if i == values_b_done:
                 previous_block_products()

from contextlib import ExitStack

import concourse.mybir as mybir
from concourse.masks import make_identity

F32 = mybir.dt.float32
BF16 = mybir.dt.bfloat16
U32 = mybir.dt.uint32
U8 = mybir.dt.uint8
FP8X4 = mybir.dt.float8_e4m3fn_x4
ALU = mybir.AluOpType
ACT = mybir.ActivationFunctionType
AXIS = mybir.AxisListType

P = 128
PACK = 4
K_PASS = P * PACK

SEQS = 4
SEQ_LEN = 128
D = 16384
FEATURES = 128
BLOCK_LEN = 4
TOKENS = SEQS * SEQ_LEN
BLOCKS = SEQ_LEN // BLOCK_LEN
WINDOWS = SEQS * BLOCKS
WINDOW = 2 * BLOCK_LEN
PASSES = D // K_PASS
CHUNK_PASSES = 4
CHUNKS = PASSES // CHUNK_PASSES
CHUNK_K = CHUNK_PASSES * K_PASS
WORDS_PASS = K_PASS // 2
TILE_PASSES = 8
BANK_PASSES = 2
TILE_BANKS = TILE_PASSES // BANK_PASSES
VECTOR_BANK = 8
NEG = -3.4028234663852886e38

FLOPS = 2 * TOKENS * D * 4 * FEATURES


def tile_tokenlevelcompressor_pa_k_kernel(tc, h, w_kv_a, w_kv_b, w_z_a, w_z_b, b_a, b_b, out):
    nc = tc.nc
    with ExitStack() as stack:
        const = stack.enter_context(tc.tile_pool(name="const", bufs=1))
        keep = stack.enter_context(tc.tile_pool(name="keep", bufs=1))
        h_in = stack.enter_context(tc.tile_pool(name="h_in", bufs=6))
        h_group = stack.enter_context(tc.tile_pool(name="h_group", bufs=6))
        w_in = stack.enter_context(tc.tile_pool(name="w_in", bufs=8))
        w_group = stack.enter_context(tc.tile_pool(name="w_group", bufs=6))
        w_packed = stack.enter_context(tc.tile_pool(name="w_packed", bufs=4))
        soft = stack.enter_context(tc.tile_pool(name="soft", bufs=1))
        sums = stack.enter_context(tc.psum_pool(name="sums", bufs=1))
        banks = stack.enter_context(tc.psum_pool(name="banks", bufs=4))
        stack.enter_context(tc.manual_schedule())

        ident = const.tile([P, P], F32)
        make_identity(nc, ident[:])

        bias_rows = const.tile([P, FEATURES], BF16)
        nc.vector.memset(bias_rows[:], 0.0)
        nc.scalar.dma_start(out=bias_rows[0:BLOCK_LEN, :], in_=b_b)
        nc.scalar.dma_start(out=bias_rows[BLOCK_LEN:WINDOW, :], in_=b_a)

        warm = const.tile([P, 1], F32)
        nc.vector.memset(warm[:], 0.0)
        nc.scalar.activation(out=warm[:], in_=warm[:], func=ACT.Exp)

        logits = soft.tile([P, SEQS, BLOCKS, WINDOW], F32)
        products_b = soft.tile([P, SEQS, BLOCKS, BLOCK_LEN], F32)
        products_a = soft.tile([P, SEQS, BLOCKS, BLOCK_LEN], F32)
        nc.vector.memset(logits[:, :, 0:1, 0:BLOCK_LEN], NEG)
        nc.vector.memset(products_b[:, :, 0:1, :], 0.0)

        h_codes = keep.tile([P, PASSES, TOKENS], U32, align_bytes=64)
        h_scales = keep.tile([P, PASSES, TOKENS], U8, align_bytes=64)

        def quantise_h_bank(b, first, h_grouped):
            tokens = slice(b * SEQ_LEN, (b + 1) * SEQ_LEN)
            for q in range(BANK_PASSES):
                nc.vector.quantize_mx(
                    out=h_codes[:, first + q, tokens].bitcast(FP8X4),
                    scales=h_scales[:, first + q, tokens],
                    in_=h_grouped[:, q].rearrange("p n t -> p (n t)"),
                )

        copied = None
        for b in range(SEQS):
            for tile_first in range(0, PASSES, TILE_PASSES):
                h_raw = h_in.tile([P, TILE_PASSES * K_PASS], BF16)
                nc.sync.dma_start(
                    out=h_raw[:], in_=h[b, :, tile_first * K_PASS : (tile_first + TILE_PASSES) * K_PASS]
                )
                words = h_raw[:].bitcast(F32)
                for bank_no in range(TILE_BANKS):
                    bank = banks.tile([P, BANK_PASSES, 2, SEQ_LEN], F32)
                    for q in range(BANK_PASSES):
                        gl = bank_no * BANK_PASSES + q
                        for u in range(2):
                            nc.tensor.transpose(
                                bank[:, q, u, :],
                                words[:, gl * WORDS_PASS + u : (gl + 1) * WORDS_PASS : 2],
                                ident[:],
                            )
                    h_grouped = h_group.tile([P, BANK_PASSES, SEQ_LEN, PACK], BF16, align_bytes=64)
                    grouped_words = (
                        h_grouped[:]
                        .rearrange("p q n t -> p (q n t)")
                        .bitcast(F32)
                        .rearrange("p (q n u) -> p q n u", q=BANK_PASSES, u=2)
                    )
                    if (tile_first // BANK_PASSES + bank_no) % VECTOR_BANK == VECTOR_BANK - 1:
                        nc.vector.tensor_copy(out=grouped_words, in_=bank[:].rearrange("p q u n -> p q n u"))
                    else:
                        nc.scalar.copy(out=grouped_words, in_=bank[:].rearrange("p q u n -> p q n u"))
                    if copied is not None:
                        quantise_h_bank(*copied)
                    copied = (b, tile_first + bank_no * BANK_PASSES, h_grouped)
        quantise_h_bank(*copied)

        bias_rows_f32 = const.tile([P, FEATURES], F32)
        nc.vector.tensor_copy(out=bias_rows_f32[:], in_=bias_rows[:])
        bias_bank = banks.tile([P, BANK_PASSES, 2, SEQ_LEN], F32, name="bank")
        nc.tensor.transpose(bias_bank[:, 0, 0, :], bias_rows_f32[:], ident[:])
        bias = const.tile([P, WINDOW], F32)

        z_a = sums.tile([P, TOKENS], F32)
        z_b = sums.tile([P, TOKENS], F32)
        c_a = sums.tile([P, TOKENS], F32)
        c_b = sums.tile([P, TOKENS], F32)
        by_block = "p (b j i) -> p b j i"
        windows = logits[:].rearrange("p b j s -> p (b j) s")
        top = soft.tile([P, WINDOWS], F32)
        expd = soft.tile([P, SEQS, BLOCKS, WINDOW], F32)
        denom = soft.tile([P, WINDOWS], F32)
        inv_denom = soft.tile([P, FEATURES], F32)

        def previous_block_logits():
            nc.vector.tensor_tensor(
                out=logits[:, :, 1:BLOCKS, 0:BLOCK_LEN],
                in0=z_b[:].rearrange(by_block, b=SEQS, i=BLOCK_LEN)[:, :, 0 : BLOCKS - 1, :],
                in1=bias[:, 0:BLOCK_LEN].unsqueeze(1).unsqueeze(1).to_broadcast([P, SEQS, BLOCKS - 1, BLOCK_LEN]),
                op=ALU.add,
            )

        def own_block_logits():
            nc.vector.tensor_tensor(
                out=logits[:, :, :, BLOCK_LEN:WINDOW],
                in0=z_a[:].rearrange(by_block, b=SEQS, i=BLOCK_LEN),
                in1=bias[:, BLOCK_LEN:WINDOW].unsqueeze(1).unsqueeze(1).to_broadcast([P, SEQS, BLOCKS, BLOCK_LEN]),
                op=ALU.add,
            )

        def largest():
            nc.vector.tensor_reduce(out=top[:], in_=windows, axis=AXIS.X, op=ALU.max)

        def shifted_logits():
            nc.vector.tensor_tensor(
                out=windows,
                in0=windows,
                in1=top[:].unsqueeze(2).to_broadcast([P, WINDOWS, WINDOW]),
                op=ALU.subtract,
            )

        def exponentials():
            nc.scalar.activation(out=expd[:], in_=logits[:], func=ACT.Exp)

        def denominators():
            nc.vector.tensor_reduce(
                out=denom[:], in_=expd[:].rearrange("p b j s -> p (b j) s"), axis=AXIS.X, op=ALU.add
            )

        def inverses():
            nc.vector.reciprocal(out=inv_denom[:], in_=denom_bank[:, 0, 0, :])

        def previous_block_products():
            nc.vector.tensor_tensor(
                out=products_b[:, :, 1:BLOCKS, :],
                in0=c_b[:].rearrange(by_block, b=SEQS, i=BLOCK_LEN)[:, :, 0 : BLOCKS - 1, :],
                in1=expd[:, :, 1:BLOCKS, 0:BLOCK_LEN],
                op=ALU.mult,
            )

        pieces = []
        for c in range(CHUNKS):
            pieces.append((z_a, w_z_a, c * CHUNK_PASSES, CHUNK_PASSES))
            pieces.append((z_b, w_z_b, c * CHUNK_PASSES, CHUNK_PASSES))
        for c in range(CHUNKS):
            pieces.append((c_b, w_kv_b, c * CHUNK_PASSES, CHUNK_PASSES))
        for c in range(CHUNKS - 1):
            pieces.append((c_a, w_kv_a, c * CHUNK_PASSES, CHUNK_PASSES))
        for first in range(PASSES - CHUNK_PASSES, PASSES, CHUNK_PASSES // 2):
            pieces.append((c_a, w_kv_a, first, CHUNK_PASSES // 2))
        logits_done = 2 * CHUNKS + 2
        values_b_done = 3 * CHUNKS + 2

        def regroup(i):
            acc, weight, first, count = pieces[i]
            w_raw = w_in.tile([P, CHUNK_PASSES, PACK * FEATURES], BF16)
            rows = weight[first * K_PASS : (first + count) * K_PASS, :]
            nc.sync.dma_start(out=w_raw[:, 0:count], in_=rows.rearrange("(g p t) n -> p g (t n)", p=P, t=PACK))
            w_grouped = w_group.tile([P, CHUNK_PASSES, FEATURES, PACK], BF16, align_bytes=64)
            if (i % 2 == 0 and i < len(pieces) - 2) or (i >= 2 * CHUNKS and i % 16 == 3) or i == len(pieces) - 2:
                for gl in range(count):
                    nc.scalar.copy(
                        out=w_grouped[:, gl].rearrange("p (c i) t -> p c t i", i=4),
                        in_=w_raw[:, gl].rearrange("p (t c i) -> p c t i", t=PACK, i=4),
                    )
            else:
                nc.vector.tensor_copy(
                    out=w_grouped[:, 0:count].rearrange("p g (c i) t -> p g c t i", i=4),
                    in_=w_raw[:, 0:count].rearrange("p g (t c i) -> p g c t i", t=PACK, i=4),
                )
            return w_grouped

        def quantise(i, w_grouped):
            count = pieces[i][3]
            w_codes = w_packed.tile([P, CHUNK_PASSES, FEATURES], U32, align_bytes=64)
            w_scales = w_packed.tile([P, CHUNK_PASSES, FEATURES], U8, align_bytes=64)
            nc.vector.quantize_mx(
                out=w_codes[:, 0:count].rearrange("p g n -> p (g n)").bitcast(FP8X4),
                scales=w_scales[:, 0:count].rearrange("p g n -> p (g n)"),
                in_=w_grouped[:, 0:count].rearrange("p g n t -> p (g n t)"),
            )
            return w_codes, w_scales

        def project(i, w_codes, w_scales):
            acc, weight, first, count = pieces[i]
            for gl in range(count):
                g = first + gl
                nc.tensor.matmul_mx(
                    out=acc[:],
                    lhsT=w_codes[:, gl, :].bitcast(FP8X4),
                    lhsT_scale=w_scales[:, gl, :],
                    rhs=h_codes[:, g, :].bitcast(FP8X4),
                    rhs_scale=h_scales[:, g, :],
                    start=(g == 0),
                    stop=(g == PASSES - 1),
                )

        grouped_of = {}
        packed_of = {}
        for i in range(len(pieces) + 2):
            if i < len(pieces):
                grouped_of[i] = regroup(i)
            if 1 <= i <= len(pieces):
                packed_of[i - 1] = quantise(i - 1, grouped_of[i - 1])
            if i >= 2:
                project(i - 2, packed_of[i - 2][0], packed_of[i - 2][1])
            if i == logits_done:
                nc.vector.tensor_copy(out=bias[:], in_=bias_bank[:, 0, 0, 0:WINDOW])
                own_block_logits()
            if i == logits_done + 1:
                previous_block_logits()
            if i == logits_done + 2:
                largest()
            if i == logits_done + 3:
                shifted_logits()
            if i == logits_done + 5:
                exponentials()
            if i == logits_done + 8:
                denominators()
            if i == logits_done + 9:
                denom_bank = banks.tile([P, BANK_PASSES, 2, SEQ_LEN], F32, name="bank")
                nc.tensor.transpose(denom_bank[:, 0, 0, :], denom[:], ident[:])
            if i == logits_done + 12:
                inverses()
            if i == values_b_done:
                previous_block_products()

        sum_b = soft.tile([P, WINDOWS], F32)
        nc.vector.tensor_reduce(
            out=sum_b[:], in_=products_b[:].rearrange("p b j i -> p (b j) i"), axis=AXIS.X, op=ALU.add
        )
        nc.vector.tensor_tensor(
            out=products_a[:],
            in0=c_a[:].rearrange(by_block, b=SEQS, i=BLOCK_LEN),
            in1=expd[:, :, :, BLOCK_LEN:WINDOW],
            op=ALU.mult,
        )
        sum_a = soft.tile([P, WINDOWS], F32)
        nc.vector.tensor_reduce(
            out=sum_a[:], in_=products_a[:].rearrange("p b j i -> p (b j) i"), axis=AXIS.X, op=ALU.add
        )
        numer = soft.tile([P, WINDOWS], F32)
        nc.vector.tensor_tensor(out=numer[:], in0=sum_a[:], in1=sum_b[:], op=ALU.add)

        result_bank = banks.tile([P, BANK_PASSES, 2, SEQ_LEN], F32, name="bank")
        nc.tensor.transpose(result_bank[:, 0, 0, :], numer[:], ident[:])
        rows_out = soft.tile([P, FEATURES], F32)
        nc.vector.tensor_tensor(out=rows_out[:], in0=result_bank[:, 0, 0, :], in1=inv_denom[:], op=ALU.mult)
        nc.sync.dma_start(out=out.rearrange("b j f -> (b j) f"), in_=rows_out[:])
